import numpy as np
import ml_dtypes


def mxq(x, axis, fmt="e4m3"):
    dtype, down = {"e4m3": (ml_dtypes.float8_e4m3fn, 7), "e5m2": (ml_dtypes.float8_e5m2, 14)}[fmt]
    v = np.moveaxis(np.asarray(x, np.float32).astype(ml_dtypes.bfloat16).astype(np.float64), axis, -1)
    blocks = v.reshape(v.shape[:-1] + (-1, 32))
    amax = np.abs(blocks).max(-1, keepdims=True)
    byte = np.maximum(np.where(amax > 0, np.frexp(amax)[1] - 1 + 127, 0) - down, 1)
    scale = np.exp2(byte - 127.0)
    codes = (blocks / scale).astype(np.float32).astype(dtype).astype(np.float64)
    return np.moveaxis((codes * scale).reshape(v.shape), -1, axis)


WIDE = False


def mx_kscale(k):
    if not WIDE:
        return np.ones(k)
    levels = np.array([10, -10, 5, -5, 0])
    a = np.random.permutation(np.resize(levels, k // 512 * 4)).reshape(k // 512, 4)
    idx = np.arange(k)
    return np.exp2(a[idx // 512, idx % 128 // 32])


BF16 = ml_dtypes.bfloat16


def bf(x):
    return np.asarray(x, np.float32).astype(BF16)


def f64(x):
    return np.asarray(x).astype(np.float64)


B, S, E, H, KV, DH = 4, 1024, 1024, 4, 1, 128
THETA = 10000.0


def rope(x):
    b, s, h, hd = x.shape
    half = hd // 2
    inv_freq = 1.0 / THETA ** (f64(np.arange(0, half, 2)) / half)
    pos = np.broadcast_to(f64(np.arange(s))[None, :], (b, s))
    freqs = pos[:, :, None] * inv_freq[None, None, :]
    cos = np.cos(freqs)[:, :, None, :]
    sin = np.sin(freqs)[:, :, None, :]
    pairs = x[..., :half].reshape(b, s, h, half // 2, 2)
    x0, x1 = pairs[..., 0], pairs[..., 1]
    rot = np.stack([x0 * cos - x1 * sin, x0 * sin + x1 * cos], axis=-1).reshape(b, s, h, half)
    return np.concatenate([rot, x[..., half:]], axis=-1)


def setup_inputs():
    s = mx_kscale(E)
    return {"hidden_states": bf(np.random.standard_normal((B, S, E)) * s),
            "Wq": bf(np.random.standard_normal((E, H * DH)) * 1.25 / np.sqrt(E) / s[:, None]),
            "Wk": bf(np.random.standard_normal((E, KV * DH)) * 1.25 / np.sqrt(E) / s[:, None]),
            "Wv": bf(np.random.standard_normal((E, KV * DH)) * 1.25 / np.sqrt(E) / s[:, None])}


def reference(hidden_states, Wq, Wk, Wv):
    xq = mxq(f64(hidden_states), 2, "e4m3")
    q = (xq @ mxq(f64(Wq), 0, "e4m3")).reshape(B, S, H, DH)
    k = (xq @ mxq(f64(Wk), 0, "e4m3")).reshape(B, S, KV, DH)
    v = (xq @ mxq(f64(Wv), 0, "e4m3")).reshape(B, S, KV, DH)
    return rope(q), rope(k), v

@@ -1,0 +1,346 @@
+import math
+from contextlib import ExitStack
+
+import concourse.mybir as mybir
+from concourse.masks import make_identity
+
+FLOPS = 2 * 4096 * 1024 * 768
+
+F32 = mybir.dt.float32
+BF16 = mybir.dt.bfloat16
+I32 = mybir.dt.int32
+U32 = mybir.dt.uint32
+U8 = mybir.dt.uint8
+FP8X4 = mybir.dt.float8_e4m3fn_x4
+ALU = mybir.AluOpType
+ACT = mybir.ActivationFunctionType
+
+P = 128
+NB = 4
+TPP = 8
+E = 1024
+NPAIR = 16
+THETA = 10000.0
+TWO_PI = 2.0 * math.pi
+C1 = 51472.0 / 8192.0
+C2 = TWO_PI - C1
+
+X_CHUNKS = [(0, 0, 2), (0, 2, 2), (0, 4, 4), (1, 0, 4), (1, 4, 4), (2, 0, 4), (2, 4, 4), (3, 0, 4), (3, 4, 4)]
+Q_GROUPS = [[0, 1], [2, 3], [4, 5], [6, 7], [8, 9], [10, 11], [12, 13], [14], [15]]
+KV_GROUPS = [[0, 1, 2, 3], [4, 5, 6, 7], [8, 9, 10, 11], [12, 13], [14], [15]]
+
+
+def tile_diffucoderattention_pa_t_kernel(tc, hidden_states, Wq, Wk, Wv, out_0, out_1, out_2):
+    nc = tc.nc
+    with ExitStack() as ctx:
+        const = ctx.enter_context(tc.tile_pool(name="const", bufs=1))
+        xin = ctx.enter_context(tc.tile_pool(name="xin", bufs=1))
+        work = ctx.enter_context(tc.tile_pool(name="work", bufs=3))
+        rope = ctx.enter_context(tc.tile_pool(name="rope", bufs=2))
+        outp = ctx.enter_context(tc.tile_pool(name="outp", bufs=4))
+        psum = ctx.enter_context(tc.psum_pool(name="psum", bufs=2))
+        ctx.enter_context(tc.manual_schedule())
+
+        wq_raw = [const.tile([P, 2048], BF16, name="wq_raw%d" % g) for g in range(2)]
+        wk_raw = const.tile([P, 1024], BF16, name="wk_raw")
+        wv_raw = const.tile([P, 1024], BF16, name="wv_raw")
+        wq_view = Wq.rearrange("(g u q e) c -> g q u (e c)", g=2, u=2, q=P, e=2)
+        for g in range(2):
+            nc.sync.dma_start(out=wq_raw[g][:].rearrange("p (u x) -> p u x", u=2), in_=wq_view[g])
+        x_tiles = []
+        x_of_pair = {}
+        for ci, (b, j0, nj) in enumerate(X_CHUNKS):
+            xt = xin.tile([P, nj * E], BF16, name="x%d" % ci)
+            x_tiles.append(xt)
+            for k in range(nj // 2):
+                x_of_pair[b * 4 + j0 // 2 + k] = (xt, 2 * k)
+
+        def load_x(ci):
+            b, j0, nj = X_CHUNKS[ci]
+            src = hidden_states[b].rearrange("(p j) e -> p (j e)", j=TPP)
+            nc.sync.dma_start(out=x_tiles[ci][:], in_=src[:, j0 * E : (j0 + nj) * E])
+
+        load_x(0)
+        nc.sync.dma_start(
+            out=wk_raw[:].rearrange("p (v x) -> p v x", v=4),
+            in_=Wk.rearrange("(v q e) c -> q v (e c)", v=4, q=P, e=2),
+        )
+        nc.sync.dma_start(
+            out=wv_raw[:].rearrange("p (v x) -> p v x", v=4),
+            in_=Wv.rearrange("(v q e) c -> q v (e c)", v=4, q=P, e=2),
+        )
+        for ci in range(1, len(X_CHUNKS)):
+            load_x(ci)
+
+        pos_i = const.tile([P, TPP], I32, name="pos_i")
+        nc.gpsimd.iota(pos_i[:], pattern=[[1, TPP]], base=0, channel_multiplier=TPP)
+        ident = const.tile([P, P], F32, name="ident")
+        make_identity(nc, ident[:])
+
+        zero1 = const.tile([P, 1], F32, name="zero1")
+        warm = const.tile([P, 1], F32, name="warm")
+        nc.vector.memset(zero1[:], 0.0)
+        nc.scalar.activation(out=warm[:], in_=zero1[:], func=ACT.Sin)
+
+        NT = TPP * 32
+        pos_f = const.tile([P, TPP], F32, name="pos_f")
+        freq = const.tile([P, 32], F32, name="freq")
+        ang = const.tile([P, NT], F32, name="ang")
+        turns_i = const.tile([P, NT], I32, name="turns_i")
+        turns = const.tile([P, NT], F32, name="turns")
+        red1 = const.tile([P, NT], F32, name="red1")
+        red = const.tile([P, NT], F32, name="red")
+        nabs = const.tile([P, NT], F32, name="nabs")
+        carg = const.tile([P, NT], F32, name="carg")
+        sin_h = const.tile([P, NT], F32, name="sin_h")
+        cos_h = const.tile([P, NT], F32, name="cos_h")
+        sq_h = const.tile([P, NT], F32, name="sq_h")
+        sin_pos = const.tile([P, TPP, 32], F32, name="sin_pos")
+        sin_neg = const.tile([P, TPP, 32], F32, name="sin_neg")
+        cos_dup = const.tile([P, TPP, 64], F32, name="cos_dup")
+
+        nc.vector.tensor_copy(out=pos_f[:], in_=pos_i[:])
+        nc.vector.memset(freq[:, 0:1], 1.0)
+        w = 1
+        while w < 32:
+            nc.vector.tensor_scalar(
+                out=freq[:, w : 2 * w], in0=freq[:, 0:w], scalar1=THETA ** (-w / 32.0), scalar2=None, op0=ALU.mult
+            )
+            w *= 2
+        nc.vector.tensor_tensor(
+            out=ang[:].rearrange("p (j i) -> p j i", j=TPP),
+            in0=pos_f[:].unsqueeze(2).to_broadcast([P, TPP, 32]),
+            in1=freq[:].unsqueeze(1).to_broadcast([P, TPP, 32]),
+            op=ALU.mult,
+        )
+        nc.vector.tensor_scalar(
+            out=turns_i[:], in0=ang[:], scalar1=1.0 / TWO_PI, scalar2=0.25, op0=ALU.mult, op1=ALU.add
+        )
+        nc.vector.tensor_copy(out=turns[:], in_=turns_i[:])
+        nc.vector.scalar_tensor_tensor(out=red1[:], in0=turns[:], scalar=-C1, in1=ang[:], op0=ALU.mult, op1=ALU.add)
+        nc.vector.scalar_tensor_tensor(out=red[:], in0=turns[:], scalar=-C2, in1=red1[:], op0=ALU.mult, op1=ALU.add)
+        nc.vector.scalar_tensor_tensor(out=nabs[:], in0=red[:], scalar=-1.0, in1=red[:], op0=ALU.mult, op1=ALU.min)
+        nc.vector.tensor_scalar(
+            out=carg[:], in0=nabs[:], scalar1=0.5, scalar2=0.5 * math.pi, op0=ALU.mult, op1=ALU.add
+        )
+        nc.scalar.activation(out=sin_h[:], in_=red[:], func=ACT.Sin, scale=0.5)
+        nc.scalar.activation(out=cos_h[:], in_=carg[:], func=ACT.Sin)
+        nc.scalar.activation(out=sq_h[:], in_=sin_h[:], func=ACT.Square)
+
+        def transposes(n):
+            xt, off = x_of_pair[n]
+            xw = xt[:].bitcast(F32)
+            banks = []
+            for a in range(2):
+                tp = psum.tile([P, 4, P], F32, name="tp%d" % a, tag="tp%d" % a, bufs=1)
+                for v in range(4):
+                    c0 = (off + a) * 512 + v * P
+                    nc.tensor.transpose(tp[:, v, :], xw[:, c0 : c0 + P], ident[:])
+                banks.append(tp)
+            return banks
+
+        def evacuate(banks):
+            xg = work.tile([P, 2048], BF16, name="xg", tag="xg", align_bytes=64)
+            xgw = xg[:].bitcast(F32).rearrange("p (a g r u) -> p a g r u", a=2, g=2, r=P, u=2)
+            for a in range(2):
+                nc.scalar.copy(out=xgw[:, a], in_=banks[a][:].rearrange("p (g u) r -> p g r u", u=2))
+            return xg
+
+        def quantise_x(xg):
+            xc = work.tile([P, 512], U32, name="xc", tag="xc", align_bytes=64)
+            xs = work.tile([P, 512], U8, name="xs", tag="xs", align_bytes=64)
+            nc.vector.quantize_mx(out=xc[:].bitcast(FP8X4), scales=xs[:], in_=xg[:])
+            return xc, xs
+
+        xg_of = {}
+        xq_of = {}
+
+        xg_of[0] = evacuate(transposes(0))
+
+        wg = const.tile([P, 2 * 768 * 4], BF16, name="wg", align_bytes=64)
+        wg_v = wg[:].rearrange("p (g c t) -> p g c t", g=2, c=768, t=4)
+        wc = const.tile([P, 2, 768], U32, name="wc", align_bytes=64)
+        ws = const.tile([P, 2, 768], U8, name="ws", align_bytes=64)
+        for g in range(2):
+            src = wq_raw[g][:].rearrange("p (t h s f) -> p s h f t", t=4, h=4, s=2, f=64)
+            for s in range(2):
+                nc.vector.tensor_copy(
+                    out=wg_v[:, g, s * 256 : (s + 1) * 256, :].rearrange("p (h f) t -> p h f t", h=4), in_=src[:, s]
+                )
+        nc.scalar.copy(out=wg_v[:, :, 512:640, :], in_=wk_raw[:].rearrange("p (g t c) -> p g c t", g=2, t=4, c=P))
+        nc.scalar.copy(out=wg_v[:, :, 640:768, :], in_=wv_raw[:].rearrange("p (g t c) -> p g c t", g=2, t=4, c=P))
+
+        def quantise_w(g, c0, c1):
+            nc.vector.quantize_mx(
+                out=wc[:, g, c0:c1].bitcast(FP8X4),
+                scales=ws[:, g, c0:c1],
+                in_=wg_v[:, g, c0:c1, :].rearrange("p c t -> p (c t)"),
+            )
+
+        quantise_w(0, 0, 512)
+        quantise_w(1, 0, 512)
+        xq_of[0] = quantise_x(xg_of[0])
+        quantise_w(0, 512, 768)
+        quantise_w(1, 512, 768)
+
+        nc.vector.scalar_tensor_tensor(
+            out=sin_pos[:].rearrange("p j i -> p (j i)"), in0=sin_h[:], scalar=2.0, in1=cos_h[:], op0=ALU.mult, op1=ALU.mult
+        )
+        nc.vector.scalar_tensor_tensor(
+            out=sin_neg[:].rearrange("p j i -> p (j i)"), in0=sin_h[:], scalar=-2.0, in1=cos_h[:], op0=ALU.mult, op1=ALU.mult
+        )
+        nc.vector.tensor_scalar(
+            out=cos_dup[:].rearrange("p j (i e) -> p (j i) e", e=2),
+            in0=sq_h[:].unsqueeze(2).to_broadcast([P, NT, 2]),
+            scalar1=-2.0,
+            scalar2=1.0,
+            op0=ALU.mult,
+            op1=ALU.add,
+        )
+
+        banks_of = {}
+        q_tile_of = {}
+        kv_tile_of = {}
+
+        def mx(n, bank, c0):
+            xc, xs = xq_of[n]
+            for a in range(2):
+                for g in range(2):
+                    blk = slice((a * 2 + g) * P, (a * 2 + g + 1) * P)
+                    nc.tensor.matmul_mx(
+                        out=bank[:, a * 256 : (a + 1) * 256],
+                        lhsT=xc[:, blk].bitcast(FP8X4),
+                        lhsT_scale=xs[:, blk],
+                        rhs=wc[:, g, c0 : c0 + 256].bitcast(FP8X4),
+                        rhs_scale=ws[:, g, c0 : c0 + 256],
+                        start=(g == 0),
+                        stop=(g == 1),
+                    )
+
+        def out_tiles(n):
+            for grp in Q_GROUPS:
+                if grp[0] == n:
+                    qo = outp.tile([P, len(grp) * 8, P], F32, name="qo", tag="qo")
+                    for k, m in enumerate(grp):
+                        q_tile_of[m] = (qo, k, grp)
+            for grp in KV_GROUPS:
+                if grp[0] == n:
+                    ko = outp.tile([P, len(grp) * 2, P], F32, name="ko", tag="ko", bufs=3)
+                    vo = outp.tile([P, len(grp) * 2, P], F32, name="vo", tag="vo", bufs=3)
+                    for k, m in enumerate(grp):
+                        kv_tile_of[m] = (ko, vo, k, grp)
+
+        def rope_q(n):
+            bank_r = banks_of[n][0]
+            j0 = 2 * (n % 4)
+            qo, k, grp = q_tile_of[n]
+            t1 = rope.tile([P, 512], F32, name="t1q", tag="t1q")
+            t2 = rope.tile([P, 2, 256], F32, name="t2q", tag="t2q")
+            nc.vector.tensor_tensor(
+                out=t1[:].rearrange("p (a h f) -> p a h f", a=2, h=4),
+                in0=bank_r[:].rearrange("p (a h f) -> p a h f", a=2, h=4),
+                in1=cos_dup[:, j0 : j0 + 2, :].unsqueeze(2).to_broadcast([P, 2, 4, 64]),
+                op=ALU.mult,
+            )
+            pairs = bank_r[:].rearrange("p (a h i e) -> p a h i e", a=2, h=4, e=2)
+            for e, tab in ((0, sin_neg), (1, sin_pos)):
+                nc.vector.tensor_tensor(
+                    out=t2[:, e, :].rearrange("p (a h i) -> p a h i", a=2, h=4),
+                    in0=pairs[:, :, :, :, 1 - e],
+                    in1=tab[:, j0 : j0 + 2, :].unsqueeze(2).to_broadcast([P, 2, 4, 32]),
+                    op=ALU.mult,
+                )
+            nc.vector.tensor_tensor(
+                out=qo[:, 8 * k : 8 * k + 8, 0:64].rearrange("p m (i e) -> p m i e", e=2),
+                in0=t1[:].rearrange("p (m i e) -> p m i e", m=8, e=2),
+                in1=t2[:].rearrange("p e (m i) -> p m i e", m=8),
+                op=ALU.add,
+            )
+
+        def rope_k(n):
+            bank_k = banks_of[n][2]
+            j0 = 2 * (n % 4)
+            ko, vo, k, grp = kv_tile_of[n]
+            t1 = rope.tile([P, 2, 64], F32, name="t1k", tag="t1k")
+            t2 = rope.tile([P, 2, 2, 32], F32, name="t2k", tag="t2k")
+            nc.vector.tensor_tensor(
+                out=t1[:],
+                in0=bank_k[:].rearrange("p (a s f) -> p a s f", a=2, s=4)[:, :, 0, :],
+                in1=cos_dup[:, j0 : j0 + 2, :],
+                op=ALU.mult,
+            )
+            pairs = bank_k[:].rearrange("p (a s i e) -> p a s i e", a=2, s=4, e=2)
+            for e, tab in ((0, sin_neg), (1, sin_pos)):
+                nc.vector.tensor_tensor(
+                    out=t2[:, e], in0=pairs[:, :, 0, :, 1 - e], in1=tab[:, j0 : j0 + 2, :], op=ALU.mult
+                )
+            nc.vector.tensor_tensor(
+                out=ko[:, 2 * k : 2 * k + 2, 0:64].rearrange("p a (i e) -> p a i e", e=2),
+                in0=t1[:].rearrange("p a (i e) -> p a i e", e=2),
+                in1=t2[:].rearrange("p e a i -> p a i e"),
+                op=ALU.add,
+            )
+
+        def copy_q(n):
+            qo, k, grp = q_tile_of[n]
+            nc.scalar.copy(
+                out=qo[:, 8 * k : 8 * k + 8, 64:128], in_=banks_of[n][1][:].rearrange("p (m f) -> p m f", m=8)
+            )
+
+        def copy_kv(n):
+            bank_k = banks_of[n][2]
+            ko, vo, k, grp = kv_tile_of[n]
+            nc.scalar.copy(
+                out=ko[:, 2 * k : 2 * k + 2, 64:128],
+                in_=bank_k[:].rearrange("p (a s f) -> p a s f", a=2, s=4)[:, :, 1, :],
+            )
+            nc.scalar.copy(
+                out=vo[:, 2 * k : 2 * k + 2, :], in_=bank_k[:].rearrange("p (a s f) -> p a s f", a=2, s=2)[:, :, 1, :]
+            )
+
+        def store_q(n):
+            qo, k, grp = q_tile_of[n]
+            if grp[-1] != n:
+                return
+            b, j0 = grp[0] // 4, 2 * (grp[0] % 4)
+            dst = out_0[b].rearrange("(p j) h d -> p (j h d)", j=TPP)
+            nc.sync.dma_start(
+                out=dst[:, j0 * 512 : (j0 + 2 * len(grp)) * 512], in_=qo[:].rearrange("p m d -> p (m d)")
+            )
+
+        def store_kv(n):
+            ko, vo, k, grp = kv_tile_of[n]
+            if grp[-1] != n:
+                return
+            b, j0 = grp[0] // 4, 2 * (grp[0] % 4)
+            for dram, sb in ((out_1, ko), (out_2, vo)):
+                dst = dram[b].rearrange("(p j) o d -> p (j o d)", j=TPP)
+                nc.sync.dma_start(
+                    out=dst[:, j0 * P : (j0 + 2 * len(grp)) * P], in_=sb[:].rearrange("p m d -> p (m d)")
+                )
+
+        for n in range(NPAIR):
+            out_tiles(n)
+            bank_r = psum.tile([P, 512], F32, name="bank_r", tag="bank_r")
+            bank_p = psum.tile([P, 512], F32, name="bank_p", tag="bank_p")
+            bank_k = psum.tile([P, 512], F32, name="bank_k", tag="bank_k")
+            banks_of[n] = (bank_r, bank_p, bank_k)
+            mx(n, bank_r, 0)
+            mx(n, bank_p, 256)
+            copy_q(n)
+            ahead = 1 if n == 0 else n + 2
+            if ahead < NPAIR:
+                xg_of[ahead] = evacuate(transposes(ahead))
+            mx(n, bank_k, 512)
+            copy_kv(n)
+            if n == 0:
+                xg_of[2] = evacuate(transposes(2))
+                rope_q(n)
+                xq_of[1] = quantise_x(xg_of[1])
+            else:
+                if n + 1 < NPAIR:
+                    xq_of[n + 1] = quantise_x(xg_of[n + 1])
+                rope_q(n)
+            store_q(n)
+            rope_k(n)
+            store_kv(n)

@@ -20,6 +20,7 @@ NB = 4
 TPP = 8
 E = 1024
 NPAIR = 16
+LOOKAHEAD = 2
 THETA = 10000.0
 TWO_PI = 2.0 * math.pi
 C1 = 51472.0 / 8192.0
@@ -35,8 +36,8 @@ def tile_diffucoderattention_pa_t_kernel(tc, hidden_states, Wq, Wk, Wv, out_0, o
     with ExitStack() as ctx:
         const = ctx.enter_context(tc.tile_pool(name="const", bufs=1))
         xin = ctx.enter_context(tc.tile_pool(name="xin", bufs=1))
-        work = ctx.enter_context(tc.tile_pool(name="work", bufs=3))
-        rope = ctx.enter_context(tc.tile_pool(name="rope", bufs=2))
+        work = ctx.enter_context(tc.tile_pool(name="work", bufs=4))
+        rope = ctx.enter_context(tc.tile_pool(name="rope", bufs=3))
         outp = ctx.enter_context(tc.tile_pool(name="outp", bufs=4))
         psum = ctx.enter_context(tc.psum_pool(name="psum", bufs=2))
         ctx.enter_context(tc.manual_schedule())
@@ -95,12 +96,15 @@ def tile_diffucoderattention_pa_t_kernel(tc, hidden_states, Wq, Wk, Wv, out_0, o
         sin_h = const.tile([P, NT], F32, name="sin_h")
         cos_h = const.tile([P, NT], F32, name="cos_h")
         sq_h = const.tile([P, NT], F32, name="sq_h")
-        sin_pos = const.tile([P, TPP, 32], F32, name="sin_pos")
-        sin_neg = const.tile([P, TPP, 32], F32, name="sin_neg")
+        sin_half = const.tile([P, NT], F32, name="sin_half")
+        sign2 = const.tile([P, 2], F32, name="sign2")
+        sin_sgn = const.tile([P, TPP, 64], F32, name="sin_sgn")
         cos_dup = const.tile([P, TPP, 64], F32, name="cos_dup")
 
         nc.vector.tensor_copy(out=pos_f[:], in_=pos_i[:])
         nc.vector.memset(freq[:, 0:1], 1.0)
+        nc.vector.memset(sign2[:, 0:1], -2.0)
+        nc.vector.memset(sign2[:, 1:2], 2.0)
         w = 1
         while w < 32:
             nc.vector.tensor_scalar(
@@ -183,11 +187,12 @@ def tile_diffucoderattention_pa_t_kernel(tc, hidden_states, Wq, Wk, Wv, out_0, o
         quantise_w(0, 512, 768)
         quantise_w(1, 512, 768)
 
-        nc.vector.scalar_tensor_tensor(
-            out=sin_pos[:].rearrange("p j i -> p (j i)"), in0=sin_h[:], scalar=2.0, in1=cos_h[:], op0=ALU.mult, op1=ALU.mult
-        )
-        nc.vector.scalar_tensor_tensor(
-            out=sin_neg[:].rearrange("p j i -> p (j i)"), in0=sin_h[:], scalar=-2.0, in1=cos_h[:], op0=ALU.mult, op1=ALU.mult
+        nc.vector.tensor_tensor(out=sin_half[:], in0=sin_h[:], in1=cos_h[:], op=ALU.mult)
+        nc.vector.tensor_tensor(
+            out=sin_sgn[:].rearrange("p j (i e) -> p (j i) e", e=2),
+            in0=sin_half[:].unsqueeze(2).to_broadcast([P, NT, 2]),
+            in1=sign2[:].unsqueeze(1).to_broadcast([P, NT, 2]),
+            op=ALU.mult,
         )
         nc.vector.tensor_scalar(
             out=cos_dup[:].rearrange("p j (i e) -> p (j i) e", e=2),
@@ -230,56 +235,65 @@ def tile_diffucoderattention_pa_t_kernel(tc, hidden_states, Wq, Wk, Wv, out_0, o
                     for k, m in enumerate(grp):
                         kv_tile_of[m] = (ko, vo, k, grp)
 
-        def rope_q(n):
-            bank_r = banks_of[n][0]
+        rope_tmp = {}
+
+        def rope_q_cos(n):
             j0 = 2 * (n % 4)
-            qo, k, grp = q_tile_of[n]
             t1 = rope.tile([P, 512], F32, name="t1q", tag="t1q")
-            t2 = rope.tile([P, 2, 256], F32, name="t2q", tag="t2q")
             nc.vector.tensor_tensor(
                 out=t1[:].rearrange("p (a h f) -> p a h f", a=2, h=4),
-                in0=bank_r[:].rearrange("p (a h f) -> p a h f", a=2, h=4),
+                in0=banks_of[n][0][:].rearrange("p (a h f) -> p a h f", a=2, h=4),
                 in1=cos_dup[:, j0 : j0 + 2, :].unsqueeze(2).to_broadcast([P, 2, 4, 64]),
                 op=ALU.mult,
             )
-            pairs = bank_r[:].rearrange("p (a h i e) -> p a h i e", a=2, h=4, e=2)
-            for e, tab in ((0, sin_neg), (1, sin_pos)):
-                nc.vector.tensor_tensor(
-                    out=t2[:, e, :].rearrange("p (a h i) -> p a h i", a=2, h=4),
-                    in0=pairs[:, :, :, :, 1 - e],
-                    in1=tab[:, j0 : j0 + 2, :].unsqueeze(2).to_broadcast([P, 2, 4, 32]),
-                    op=ALU.mult,
-                )
+            rope_tmp[("q", n)] = t1
+
+        def rope_q_sin(n):
+            j0 = 2 * (n % 4)
+            t2 = rope.tile([P, 512], F32, name="t2q", tag="t2q")
             nc.vector.tensor_tensor(
-                out=qo[:, 8 * k : 8 * k + 8, 0:64].rearrange("p m (i e) -> p m i e", e=2),
-                in0=t1[:].rearrange("p (m i e) -> p m i e", m=8, e=2),
-                in1=t2[:].rearrange("p e (m i) -> p m i e", m=8),
+                out=t2[:].rearrange("p (a h i e) -> p a h i e", a=2, h=4, e=2),
+                in0=banks_of[n][0][:].rearrange("p (a h i e) -> p a h i e", a=2, h=4, e=2)[:, :, :, :, ::-1],
+                in1=sin_sgn[:, j0 : j0 + 2, :]
+                .rearrange("p a (i e) -> p a i e", e=2)
+                .unsqueeze(2)
+                .to_broadcast([P, 2, 4, 32, 2]),
+                op=ALU.mult,
+            )
+            return t2
+
+        def rope_q_add(n, t2, eng):
+            qo, k, grp = q_tile_of[n]
+            eng.tensor_tensor(
+                out=qo[:, 8 * k : 8 * k + 8, 0:64],
+                in0=rope_tmp[("q", n)][:].rearrange("p (m f) -> p m f", m=8),
+                in1=t2[:].rearrange("p (m f) -> p m f", m=8),
                 op=ALU.add,
             )
 
-        def rope_k(n):
+        def rope_k_mul(n):
             bank_k = banks_of[n][2]
             j0 = 2 * (n % 4)
-            ko, vo, k, grp = kv_tile_of[n]
             t1 = rope.tile([P, 2, 64], F32, name="t1k", tag="t1k")
-            t2 = rope.tile([P, 2, 2, 32], F32, name="t2k", tag="t2k")
+            t2 = rope.tile([P, 2, 64], F32, name="t2k", tag="t2k")
             nc.vector.tensor_tensor(
                 out=t1[:],
                 in0=bank_k[:].rearrange("p (a s f) -> p a s f", a=2, s=4)[:, :, 0, :],
                 in1=cos_dup[:, j0 : j0 + 2, :],
                 op=ALU.mult,
             )
-            pairs = bank_k[:].rearrange("p (a s i e) -> p a s i e", a=2, s=4, e=2)
-            for e, tab in ((0, sin_neg), (1, sin_pos)):
-                nc.vector.tensor_tensor(
-                    out=t2[:, e], in0=pairs[:, :, 0, :, 1 - e], in1=tab[:, j0 : j0 + 2, :], op=ALU.mult
-                )
             nc.vector.tensor_tensor(
-                out=ko[:, 2 * k : 2 * k + 2, 0:64].rearrange("p a (i e) -> p a i e", e=2),
-                in0=t1[:].rearrange("p a (i e) -> p a i e", e=2),
-                in1=t2[:].rearrange("p e a i -> p a i e"),
-                op=ALU.add,
+                out=t2[:].rearrange("p a (i e) -> p a i e", e=2),
+                in0=bank_k[:].rearrange("p (a s i e) -> p a s i e", a=2, s=4, e=2)[:, :, 0, :, ::-1],
+                in1=sin_sgn[:, j0 : j0 + 2, :].rearrange("p a (i e) -> p a i e", e=2),
+                op=ALU.mult,
             )
+            rope_tmp[("k", n)] = (t1, t2)
+
+        def rope_k_add(n):
+            ko, vo, k, grp = kv_tile_of[n]
+            t1, t2 = rope_tmp[("k", n)]
+            nc.vector.tensor_tensor(out=ko[:, 2 * k : 2 * k + 2, 0:64], in0=t1[:], in1=t2[:], op=ALU.add)
 
         def copy_q(n):
             qo, k, grp = q_tile_of[n]
@@ -319,6 +333,8 @@ def tile_diffucoderattention_pa_t_kernel(tc, hidden_states, Wq, Wk, Wv, out_0, o
                     out=dst[:, j0 * P : (j0 + 2 * len(grp)) * P], in_=sb[:].rearrange("p m d -> p (m d)")
                 )
 
+        next_t = 1
+        next_q = 1
         for n in range(NPAIR):
             out_tiles(n)
             bank_r = psum.tile([P, 512], F32, name="bank_r", tag="bank_r")
@@ -328,19 +344,26 @@ def tile_diffucoderattention_pa_t_kernel(tc, hidden_states, Wq, Wk, Wv, out_0, o
             mx(n, bank_r, 0)
             mx(n, bank_p, 256)
             copy_q(n)
-            ahead = 1 if n == 0 else n + 2
-            if ahead < NPAIR:
-                xg_of[ahead] = evacuate(transposes(ahead))
+            if next_t < NPAIR:
+                xg_of[next_t] = evacuate(transposes(next_t))
+                next_t += 1
             mx(n, bank_k, 512)
             copy_kv(n)
             if n == 0:
-                xg_of[2] = evacuate(transposes(2))
-                rope_q(n)
-                xq_of[1] = quantise_x(xg_of[1])
-            else:
-                if n + 1 < NPAIR:
-                    xq_of[n + 1] = quantise_x(xg_of[n + 1])
-                rope_q(n)
+                for extra in range(LOOKAHEAD):
+                    xg_of[next_t] = evacuate(transposes(next_t))
+                    next_t += 1
+            rope_q_cos(n)
+            for extra in range(LOOKAHEAD if n == 0 else 1):
+                if next_q < NPAIR:
+                    xq_of[next_q] = quantise_x(xg_of[next_q])
+                    next_q += 1
+            if n > 0:
+                rope_k_add(n - 1)
+                store_kv(n - 1)
+            t2 = rope_q_sin(n)
+            rope_q_add(n, t2, nc.vector if n == NPAIR - 1 else nc.gpsimd)
             store_q(n)
-            rope_k(n)
-            store_kv(n)
+            rope_k_mul(n)
+        rope_k_add(NPAIR - 1)
+        store_kv(NPAIR - 1)

@@ -354,6 +354,9 @@ def tile_diffucoderattention_pa_t_kernel(tc, hidden_states, Wq, Wk, Wv, out_0, o
                     xg_of[next_t] = evacuate(transposes(next_t))
                     next_t += 1
             rope_q_cos(n)
+            t2 = rope_q_sin(n)
+            rope_q_add(n, t2, nc.vector if n == NPAIR - 1 else nc.gpsimd)
+            store_q(n)
             for extra in range(LOOKAHEAD if n == 0 else 1):
                 if next_q < NPAIR:
                     xq_of[next_q] = quantise_x(xg_of[next_q])
@@ -361,9 +364,6 @@ def tile_diffucoderattention_pa_t_kernel(tc, hidden_states, Wq, Wk, Wv, out_0, o
             if n > 0:
                 rope_k_add(n - 1)
                 store_kv(n - 1)
-            t2 = rope_q_sin(n)
-            rope_q_add(n, t2, nc.vector if n == NPAIR - 1 else nc.gpsimd)
-            store_q(n)
             rope_k_mul(n)
         rope_k_add(NPAIR - 1)
         store_kv(NPAIR - 1)

@@ -98,13 +98,12 @@ def tile_diffucoderattention_pa_t_kernel(tc, hidden_states, Wq, Wk, Wv, out_0, o
         sq_h = const.tile([P, NT], F32, name="sq_h")
         sin_half = const.tile([P, NT], F32, name="sin_half")
         sign2 = const.tile([P, 2], F32, name="sign2")
-        sin_sgn = const.tile([P, TPP, 64], F32, name="sin_sgn")
-        cos_dup = const.tile([P, TPP, 64], F32, name="cos_dup")
+        tab = const.tile([P, 4, 2, 2, 64], F32, name="tab")
 
         nc.vector.tensor_copy(out=pos_f[:], in_=pos_i[:])
         nc.vector.memset(freq[:, 0:1], 1.0)
-        nc.vector.memset(sign2[:, 0:1], -2.0)
-        nc.vector.memset(sign2[:, 1:2], 2.0)
+        nc.vector.memset(sign2[:, 0:1], 2.0)
+        nc.vector.memset(sign2[:, 1:2], -2.0)
         w = 1
         while w < 32:
             nc.vector.tensor_scalar(
@@ -189,14 +188,14 @@ def tile_diffucoderattention_pa_t_kernel(tc, hidden_states, Wq, Wk, Wv, out_0, o
 
         nc.vector.tensor_tensor(out=sin_half[:], in0=sin_h[:], in1=cos_h[:], op=ALU.mult)
         nc.vector.tensor_tensor(
-            out=sin_sgn[:].rearrange("p j (i e) -> p (j i) e", e=2),
-            in0=sin_half[:].unsqueeze(2).to_broadcast([P, NT, 2]),
-            in1=sign2[:].unsqueeze(1).to_broadcast([P, NT, 2]),
+            out=tab[:, :, 1].rearrange("p q a (i e) -> p q (a i) e", e=2),
+            in0=sin_half[:].rearrange("p (q x) -> p q x", q=4).unsqueeze(3).to_broadcast([P, 4, 64, 2]),
+            in1=sign2[:].unsqueeze(1).unsqueeze(1).to_broadcast([P, 4, 64, 2]),
             op=ALU.mult,
         )
         nc.vector.tensor_scalar(
-            out=cos_dup[:].rearrange("p j (i e) -> p (j i) e", e=2),
-            in0=sq_h[:].unsqueeze(2).to_broadcast([P, NT, 2]),
+            out=tab[:, :, 0].rearrange("p q a (i e) -> p q (a i) e", e=2),
+            in0=sq_h[:].rearrange("p (q x) -> p q x", q=4).unsqueeze(3).to_broadcast([P, 4, 64, 2]),
             scalar1=-2.0,
             scalar2=1.0,
             op0=ALU.mult,
@@ -237,63 +236,51 @@ def tile_diffucoderattention_pa_t_kernel(tc, hidden_states, Wq, Wk, Wv, out_0, o
 
         rope_tmp = {}
 
-        def rope_q_cos(n):
-            j0 = 2 * (n % 4)
-            t1 = rope.tile([P, 512], F32, name="t1q", tag="t1q")
+        def rope_q_mul(n):
+            t12 = rope.tile([P, 2, 512], F32, name="t12q", tag="t12q")
             nc.vector.tensor_tensor(
-                out=t1[:].rearrange("p (a h f) -> p a h f", a=2, h=4),
-                in0=banks_of[n][0][:].rearrange("p (a h f) -> p a h f", a=2, h=4),
-                in1=cos_dup[:, j0 : j0 + 2, :].unsqueeze(2).to_broadcast([P, 2, 4, 64]),
+                out=t12[:].rearrange("p c (a h f) -> p c a h f", a=2, h=4),
+                in0=banks_of[n][0][:]
+                .rearrange("p (a h f) -> p a h f", a=2, h=4)
+                .unsqueeze(1)
+                .to_broadcast([P, 2, 2, 4, 64]),
+                in1=tab[:, n % 4].unsqueeze(3).to_broadcast([P, 2, 2, 4, 64]),
                 op=ALU.mult,
             )
-            rope_tmp[("q", n)] = t1
+            rope_tmp[("q", n)] = t12
 
-        def rope_q_sin(n):
-            j0 = 2 * (n % 4)
-            t2 = rope.tile([P, 512], F32, name="t2q", tag="t2q")
-            nc.vector.tensor_tensor(
-                out=t2[:].rearrange("p (a h i e) -> p a h i e", a=2, h=4, e=2),
-                in0=banks_of[n][0][:].rearrange("p (a h i e) -> p a h i e", a=2, h=4, e=2)[:, :, :, :, ::-1],
-                in1=sin_sgn[:, j0 : j0 + 2, :]
-                .rearrange("p a (i e) -> p a i e", e=2)
-                .unsqueeze(2)
-                .to_broadcast([P, 2, 4, 32, 2]),
-                op=ALU.mult,
-            )
-            return t2
-
-        def rope_q_add(n, t2, eng):
+        def rope_q_add(n, eng):
             qo, k, grp = q_tile_of[n]
+            t12 = rope_tmp[("q", n)]
             eng.tensor_tensor(
-                out=qo[:, 8 * k : 8 * k + 8, 0:64],
-                in0=rope_tmp[("q", n)][:].rearrange("p (m f) -> p m f", m=8),
-                in1=t2[:].rearrange("p (m f) -> p m f", m=8),
+                out=qo[:, 8 * k : 8 * k + 8, 0:64].rearrange("p m (i e) -> p m i e", e=2),
+                in0=t12[:, 0].rearrange("p (m i e) -> p m i e", m=8, e=2),
+                in1=t12[:, 1].rearrange("p (m i e) -> p m i e", m=8, e=2)[:, :, :, ::-1],
                 op=ALU.add,
             )
 
         def rope_k_mul(n):
-            bank_k = banks_of[n][2]
-            j0 = 2 * (n % 4)
-            t1 = rope.tile([P, 2, 64], F32, name="t1k", tag="t1k")
-            t2 = rope.tile([P, 2, 64], F32, name="t2k", tag="t2k")
+            t12 = rope.tile([P, 2, 2, 64], F32, name="t12k", tag="t12k")
             nc.vector.tensor_tensor(
-                out=t1[:],
-                in0=bank_k[:].rearrange("p (a s f) -> p a s f", a=2, s=4)[:, :, 0, :],
-                in1=cos_dup[:, j0 : j0 + 2, :],
+                out=t12[:],
+                in0=banks_of[n][2][:]
+                .rearrange("p (a s f) -> p a s f", a=2, s=4)[:, :, 0, :]
+                .unsqueeze(1)
+                .to_broadcast([P, 2, 2, 64]),
+                in1=tab[:, n % 4],
                 op=ALU.mult,
             )
-            nc.vector.tensor_tensor(
-                out=t2[:].rearrange("p a (i e) -> p a i e", e=2),
-                in0=bank_k[:].rearrange("p (a s i e) -> p a s i e", a=2, s=4, e=2)[:, :, 0, :, ::-1],
-                in1=sin_sgn[:, j0 : j0 + 2, :].rearrange("p a (i e) -> p a i e", e=2),
-                op=ALU.mult,
-            )
-            rope_tmp[("k", n)] = (t1, t2)
+            rope_tmp[("k", n)] = t12
 
         def rope_k_add(n):
             ko, vo, k, grp = kv_tile_of[n]
-            t1, t2 = rope_tmp[("k", n)]
-            nc.vector.tensor_tensor(out=ko[:, 2 * k : 2 * k + 2, 0:64], in0=t1[:], in1=t2[:], op=ALU.add)
+            t12 = rope_tmp[("k", n)]
+            nc.vector.tensor_tensor(
+                out=ko[:, 2 * k : 2 * k + 2, 0:64].rearrange("p a (i e) -> p a i e", e=2),
+                in0=t12[:, 0].rearrange("p a (i e) -> p a i e", e=2),
+                in1=t12[:, 1].rearrange("p a (i e) -> p a i e", e=2)[:, :, :, ::-1],
+                op=ALU.add,
+            )
 
         def copy_q(n):
             qo, k, grp = q_tile_of[n]
@@ -353,9 +340,8 @@ def tile_diffucoderattention_pa_t_kernel(tc, hidden_states, Wq, Wk, Wv, out_0, o
                 for extra in range(LOOKAHEAD):
                     xg_of[next_t] = evacuate(transposes(next_t))
                     next_t += 1
-            rope_q_cos(n)
-            t2 = rope_q_sin(n)
-            rope_q_add(n, t2, nc.vector if n == NPAIR - 1 else nc.gpsimd)
+            rope_q_mul(n)
+            rope_q_add(n, nc.vector if n == NPAIR - 1 else nc.gpsimd)
             store_q(n)
             for extra in range(LOOKAHEAD if n == 0 else 1):
                 if next_q < NPAIR:

@@ -183,8 +183,6 @@ def tile_diffucoderattention_pa_t_kernel(tc, hidden_states, Wq, Wk, Wv, out_0, o
         quantise_w(0, 0, 512)
         quantise_w(1, 0, 512)
         xq_of[0] = quantise_x(xg_of[0])
-        quantise_w(0, 512, 768)
-        quantise_w(1, 512, 768)
 
         nc.vector.tensor_tensor(out=sin_half[:], in0=sin_h[:], in1=cos_h[:], op=ALU.mult)
         nc.vector.tensor_tensor(
@@ -201,6 +199,9 @@ def tile_diffucoderattention_pa_t_kernel(tc, hidden_states, Wq, Wk, Wv, out_0, o
             op0=ALU.mult,
             op1=ALU.add,
         )
+
+        quantise_w(0, 512, 768)
+        quantise_w(1, 512, 768)
 
         banks_of = {}
         q_tile_of = {}
@@ -341,7 +342,7 @@ def tile_diffucoderattention_pa_t_kernel(tc, hidden_states, Wq, Wk, Wv, out_0, o
                     xg_of[next_t] = evacuate(transposes(next_t))
                     next_t += 1
             rope_q_mul(n)
-            rope_q_add(n, nc.vector if n == NPAIR - 1 else nc.gpsimd)
+            rope_q_add(n, nc.vector if n % 4 == 3 else nc.gpsimd)
             store_q(n)
             for extra in range(LOOKAHEAD if n == 0 else 1):
                 if next_q < NPAIR:

@@ -40,7 +40,6 @@ def tile_diffucoderattention_pa_t_kernel(tc, hidden_states, Wq, Wk, Wv, out_0, o
         rope = ctx.enter_context(tc.tile_pool(name="rope", bufs=3))
         outp = ctx.enter_context(tc.tile_pool(name="outp", bufs=4))
         psum = ctx.enter_context(tc.psum_pool(name="psum", bufs=2))
-        ctx.enter_context(tc.manual_schedule())
 
         wq_raw = [const.tile([P, 2048], BF16, name="wq_raw%d" % g) for g in range(2)]
         wk_raw = const.tile([P, 1024], BF16, name="wk_raw")

@@ -20,7 +20,6 @@ NB = 4
 TPP = 8
 E = 1024
 NPAIR = 16
-LOOKAHEAD = 2
 THETA = 10000.0
 TWO_PI = 2.0 * math.pi
 C1 = 51472.0 / 8192.0
@@ -40,6 +39,7 @@ def tile_diffucoderattention_pa_t_kernel(tc, hidden_states, Wq, Wk, Wv, out_0, o
         rope = ctx.enter_context(tc.tile_pool(name="rope", bufs=3))
         outp = ctx.enter_context(tc.tile_pool(name="outp", bufs=4))
         psum = ctx.enter_context(tc.psum_pool(name="psum", bufs=2))
+        ctx.enter_context(tc.manual_schedule())
 
         wq_raw = [const.tile([P, 2048], BF16, name="wq_raw%d" % g) for g in range(2)]
         wk_raw = const.tile([P, 1024], BF16, name="wk_raw")
@@ -61,6 +61,7 @@ def tile_diffucoderattention_pa_t_kernel(tc, hidden_states, Wq, Wk, Wv, out_0, o
             nc.sync.dma_start(out=x_tiles[ci][:], in_=src[:, j0 * E : (j0 + nj) * E])
 
         load_x(0)
+        load_x(1)
         nc.sync.dma_start(
             out=wk_raw[:].rearrange("p (v x) -> p v x", v=4),
             in_=Wk.rearrange("(v q e) c -> q v (e c)", v=4, q=P, e=2),
@@ -69,7 +70,7 @@ def tile_diffucoderattention_pa_t_kernel(tc, hidden_states, Wq, Wk, Wv, out_0, o
             out=wv_raw[:].rearrange("p (v x) -> p v x", v=4),
             in_=Wv.rearrange("(v q e) c -> q v (e c)", v=4, q=P, e=2),
         )
-        for ci in range(1, len(X_CHUNKS)):
+        for ci in range(2, len(X_CHUNKS)):
             load_x(ci)
 
         pos_i = const.tile([P, TPP], I32, name="pos_i")
@@ -157,20 +158,19 @@ def tile_diffucoderattention_pa_t_kernel(tc, hidden_states, Wq, Wk, Wv, out_0, o
         xg_of = {}
         xq_of = {}
 
-        xg_of[0] = evacuate(transposes(0))
-
         wg = const.tile([P, 2 * 768 * 4], BF16, name="wg", align_bytes=64)
         wg_v = wg[:].rearrange("p (g c t) -> p g c t", g=2, c=768, t=4)
         wc = const.tile([P, 2, 768], U32, name="wc", align_bytes=64)
         ws = const.tile([P, 2, 768], U8, name="ws", align_bytes=64)
-        for g in range(2):
+
+        def regroup_q(copy, g, s):
             src = wq_raw[g][:].rearrange("p (t h s f) -> p s h f t", t=4, h=4, s=2, f=64)
-            for s in range(2):
-                nc.vector.tensor_copy(
-                    out=wg_v[:, g, s * 256 : (s + 1) * 256, :].rearrange("p (h f) t -> p h f t", h=4), in_=src[:, s]
-                )
-        nc.scalar.copy(out=wg_v[:, :, 512:640, :], in_=wk_raw[:].rearrange("p (g t c) -> p g c t", g=2, t=4, c=P))
-        nc.scalar.copy(out=wg_v[:, :, 640:768, :], in_=wv_raw[:].rearrange("p (g t c) -> p g c t", g=2, t=4, c=P))
+            copy(out=wg_v[:, g, s * 256 : (s + 1) * 256, :].rearrange("p (h f) t -> p h f t", h=4), in_=src[:, s])
+
+        def regroup_kv(raw, c0):
+            nc.vector.tensor_copy(
+                out=wg_v[:, :, c0 : c0 + P, :], in_=raw[:].rearrange("p (g t c) -> p g c t", g=2, t=4, c=P)
+            )
 
         def quantise_w(g, c0, c1):
             nc.vector.quantize_mx(
@@ -179,17 +179,29 @@ def tile_diffucoderattention_pa_t_kernel(tc, hidden_states, Wq, Wk, Wv, out_0, o
                 in_=wg_v[:, g, c0:c1, :].rearrange("p c t -> p (c t)"),
             )
 
-        quantise_w(0, 0, 512)
-        quantise_w(1, 0, 512)
-        xq_of[0] = quantise_x(xg_of[0])
-
+        regroup_q(nc.vector.tensor_copy, 0, 0)
+        regroup_q(nc.scalar.copy, 0, 1)
         nc.vector.tensor_tensor(out=sin_half[:], in0=sin_h[:], in1=cos_h[:], op=ALU.mult)
+        regroup_q(nc.vector.tensor_copy, 1, 0)
+        regroup_q(nc.scalar.copy, 1, 1)
+        xg_of[0] = evacuate(transposes(0))
+        xg_of[1] = evacuate(transposes(1))
+        quantise_w(0, 0, 256)
+        quantise_w(1, 0, 256)
+        quantise_w(0, 256, 512)
+        quantise_w(1, 256, 512)
         nc.vector.tensor_tensor(
             out=tab[:, :, 1].rearrange("p q a (i e) -> p q (a i) e", e=2),
             in0=sin_half[:].rearrange("p (q x) -> p q x", q=4).unsqueeze(3).to_broadcast([P, 4, 64, 2]),
             in1=sign2[:].unsqueeze(1).unsqueeze(1).to_broadcast([P, 4, 64, 2]),
             op=ALU.mult,
         )
+        xq_of[0] = quantise_x(xg_of[0])
+        regroup_kv(wk_raw, 512)
+        xq_of[1] = quantise_x(xg_of[1])
+        regroup_kv(wv_raw, 640)
+        quantise_w(0, 512, 768)
+        quantise_w(1, 512, 768)
         nc.vector.tensor_scalar(
             out=tab[:, :, 0].rearrange("p q a (i e) -> p q (a i) e", e=2),
             in0=sq_h[:].rearrange("p (q x) -> p q x", q=4).unsqueeze(3).to_broadcast([P, 4, 64, 2]),
@@ -198,9 +210,6 @@ def tile_diffucoderattention_pa_t_kernel(tc, hidden_states, Wq, Wk, Wv, out_0, o
             op0=ALU.mult,
             op1=ALU.add,
         )
-
-        quantise_w(0, 512, 768)
-        quantise_w(1, 512, 768)
 
         banks_of = {}
         q_tile_of = {}
@@ -249,14 +258,23 @@ def tile_diffucoderattention_pa_t_kernel(tc, hidden_states, Wq, Wk, Wv, out_0, o
             )
             rope_tmp[("q", n)] = t12
 
-        def rope_q_add(n, eng):
+        def rope_q_add(n, eng, m0=0, m1=8):
             qo, k, grp = q_tile_of[n]
             t12 = rope_tmp[("q", n)]
             eng.tensor_tensor(
-                out=qo[:, 8 * k : 8 * k + 8, 0:64].rearrange("p m (i e) -> p m i e", e=2),
-                in0=t12[:, 0].rearrange("p (m i e) -> p m i e", m=8, e=2),
-                in1=t12[:, 1].rearrange("p (m i e) -> p m i e", m=8, e=2)[:, :, :, ::-1],
+                out=qo[:, 8 * k + m0 : 8 * k + m1, 0:64].rearrange("p m (i e) -> p m i e", e=2),
+                in0=t12[:, 0].rearrange("p (m i e) -> p m i e", m=8, e=2)[:, m0:m1],
+                in1=t12[:, 1].rearrange("p (m i e) -> p m i e", m=8, e=2)[:, m0:m1, :, ::-1],
                 op=ALU.add,
+            )
+
+        def store_q_tile(n, a):
+            qo, k, grp = q_tile_of[n]
+            b, j = n // 4, 2 * (n % 4) + a
+            dst = out_0[b].rearrange("(p j) h d -> p (j h d)", j=TPP)
+            nc.sync.dma_start(
+                out=dst[:, j * 512 : (j + 1) * 512],
+                in_=qo[:, 8 * k + 4 * a : 8 * k + 4 * a + 4, :].rearrange("p m d -> p (m d)"),
             )
 
         def rope_k_mul(n):
@@ -271,6 +289,11 @@ def tile_diffucoderattention_pa_t_kernel(tc, hidden_states, Wq, Wk, Wv, out_0, o
                 op=ALU.mult,
             )
             rope_tmp[("k", n)] = t12
+            ko, vo, k, grp = kv_tile_of[n]
+            nc.vector.tensor_copy(
+                out=ko[:, 2 * k : 2 * k + 2, 64:128],
+                in_=banks_of[n][2][:].rearrange("p (a s f) -> p a s f", a=2, s=4)[:, :, 1, :],
+            )
 
         def rope_k_add(n):
             ko, vo, k, grp = kv_tile_of[n]
@@ -291,10 +314,6 @@ def tile_diffucoderattention_pa_t_kernel(tc, hidden_states, Wq, Wk, Wv, out_0, o
         def copy_kv(n):
             bank_k = banks_of[n][2]
             ko, vo, k, grp = kv_tile_of[n]
-            nc.scalar.copy(
-                out=ko[:, 2 * k : 2 * k + 2, 64:128],
-                in_=bank_k[:].rearrange("p (a s f) -> p a s f", a=2, s=4)[:, :, 1, :],
-            )
             nc.scalar.copy(
                 out=vo[:, 2 * k : 2 * k + 2, :], in_=bank_k[:].rearrange("p (a s f) -> p a s f", a=2, s=2)[:, :, 1, :]
             )
@@ -320,36 +339,64 @@ def tile_diffucoderattention_pa_t_kernel(tc, hidden_states, Wq, Wk, Wv, out_0, o
                     out=dst[:, j0 * P : (j0 + 2 * len(grp)) * P], in_=sb[:].rearrange("p m d -> p (m d)")
                 )
 
-        next_t = 1
-        next_q = 1
-        for n in range(NPAIR):
+        def new_banks(n):
             out_tiles(n)
             bank_r = psum.tile([P, 512], F32, name="bank_r", tag="bank_r")
             bank_p = psum.tile([P, 512], F32, name="bank_p", tag="bank_p")
             bank_k = psum.tile([P, 512], F32, name="bank_k", tag="bank_k")
             banks_of[n] = (bank_r, bank_p, bank_k)
-            mx(n, bank_r, 0)
-            mx(n, bank_p, 256)
+
+        def mx_q(n):
+            mx(n, banks_of[n][0], 0)
+            mx(n, banks_of[n][1], 256)
             copy_q(n)
-            if next_t < NPAIR:
-                xg_of[next_t] = evacuate(transposes(next_t))
-                next_t += 1
-            mx(n, bank_k, 512)
+
+        def mx_kv(n):
+            mx(n, banks_of[n][2], 512)
             copy_kv(n)
-            if n == 0:
-                for extra in range(LOOKAHEAD):
-                    xg_of[next_t] = evacuate(transposes(next_t))
-                    next_t += 1
+
+        def ahead(n):
+            if n < NPAIR:
+                xg_of[n] = evacuate(transposes(n))
+
+        def vector_part(n):
             rope_q_mul(n)
-            rope_q_add(n, nc.vector if n % 4 == 3 else nc.gpsimd)
+            rope_q_add(n, nc.gpsimd)
             store_q(n)
-            for extra in range(LOOKAHEAD if n == 0 else 1):
-                if next_q < NPAIR:
-                    xq_of[next_q] = quantise_x(xg_of[next_q])
-                    next_q += 1
+            if n + 2 < NPAIR:
+                xq_of[n + 2] = quantise_x(xg_of[n + 2])
             if n > 0:
                 rope_k_add(n - 1)
                 store_kv(n - 1)
             rope_k_mul(n)
-        rope_k_add(NPAIR - 1)
-        store_kv(NPAIR - 1)
+
+        new_banks(0)
+        new_banks(1)
+        mx_q(0)
+        mx_q(1)
+        ahead(2)
+        mx_kv(0)
+        mx_kv(1)
+        ahead(3)
+        vector_part(0)
+        vector_part(1)
+        for n in range(2, NPAIR - 1):
+            new_banks(n)
+            mx_q(n)
+            ahead(n + 2)
+            mx_kv(n)
+            vector_part(n)
+
+        last = NPAIR - 1
+        new_banks(last)
+        mx_kv(last)
+        mx_q(last)
+        rope_k_add(last - 1)
+        store_kv(last - 1)
+        rope_k_mul(last)
+        rope_k_add(last)
+        store_kv(last)
+        rope_q_mul(last)
+        for a in range(2):
+            rope_q_add(last, nc.vector, 4 * a, 4 * a + 4)
+            store_q_tile(last, a)

import math
from contextlib import ExitStack

import concourse.mybir as mybir
from concourse.masks import make_identity

FLOPS = 2 * 4096 * 1024 * 768

F32 = mybir.dt.float32
BF16 = mybir.dt.bfloat16
I32 = mybir.dt.int32
U32 = mybir.dt.uint32
U8 = mybir.dt.uint8
FP8X4 = mybir.dt.float8_e4m3fn_x4
ALU = mybir.AluOpType
ACT = mybir.ActivationFunctionType

P = 128
NB = 4
TPP = 8
E = 1024
NPAIR = 16
THETA = 10000.0
TWO_PI = 2.0 * math.pi
C1 = 51472.0 / 8192.0
C2 = TWO_PI - C1

X_CHUNKS = [(0, 0, 2), (0, 2, 2), (0, 4, 4), (1, 0, 4), (1, 4, 4), (2, 0, 4), (2, 4, 4), (3, 0, 4), (3, 4, 4)]
Q_GROUPS = [[0, 1], [2, 3], [4, 5], [6, 7], [8, 9], [10, 11], [12, 13], [14], [15]]
KV_GROUPS = [[0, 1, 2, 3], [4, 5, 6, 7], [8, 9, 10, 11], [12, 13], [14], [15]]


def tile_diffucoderattention_pa_t_kernel(tc, hidden_states, Wq, Wk, Wv, out_0, out_1, out_2):
    nc = tc.nc
    with ExitStack() as ctx:
        const = ctx.enter_context(tc.tile_pool(name="const", bufs=1))
        xin = ctx.enter_context(tc.tile_pool(name="xin", bufs=1))
        work = ctx.enter_context(tc.tile_pool(name="work", bufs=4))
        rope = ctx.enter_context(tc.tile_pool(name="rope", bufs=3))
        outp = ctx.enter_context(tc.tile_pool(name="outp", bufs=4))
        psum = ctx.enter_context(tc.psum_pool(name="psum", bufs=2))
        ctx.enter_context(tc.manual_schedule())

        wq_raw = [const.tile([P, 2048], BF16, name="wq_raw%d" % g) for g in range(2)]
        wk_raw = const.tile([P, 1024], BF16, name="wk_raw")
        wv_raw = const.tile([P, 1024], BF16, name="wv_raw")
        wq_view = Wq.rearrange("(g u q e) c -> g q u (e c)", g=2, u=2, q=P, e=2)
        for g in range(2):
            nc.sync.dma_start(out=wq_raw[g][:].rearrange("p (u x) -> p u x", u=2), in_=wq_view[g])
        x_tiles = []
        x_of_pair = {}
        for ci, (b, j0, nj) in enumerate(X_CHUNKS):
            xt = xin.tile([P, nj * E], BF16, name="x%d" % ci)
            x_tiles.append(xt)
            for k in range(nj // 2):
                x_of_pair[b * 4 + j0 // 2 + k] = (xt, 2 * k)

        def load_x(ci):
            b, j0, nj = X_CHUNKS[ci]
            src = hidden_states[b].rearrange("(p j) e -> p (j e)", j=TPP)
            nc.sync.dma_start(out=x_tiles[ci][:], in_=src[:, j0 * E : (j0 + nj) * E])

        load_x(0)
        load_x(1)
        nc.sync.dma_start(
            out=wk_raw[:].rearrange("p (v x) -> p v x", v=4),
            in_=Wk.rearrange("(v q e) c -> q v (e c)", v=4, q=P, e=2),
        )
        nc.sync.dma_start(
            out=wv_raw[:].rearrange("p (v x) -> p v x", v=4),
            in_=Wv.rearrange("(v q e) c -> q v (e c)", v=4, q=P, e=2),
        )
        for ci in range(2, len(X_CHUNKS)):
            load_x(ci)

        pos_i = const.tile([P, TPP], I32, name="pos_i")
        nc.gpsimd.iota(pos_i[:], pattern=[[1, TPP]], base=0, channel_multiplier=TPP)
        ident = const.tile([P, P], F32, name="ident")
        make_identity(nc, ident[:])

        zero1 = const.tile([P, 1], F32, name="zero1")
        warm = const.tile([P, 1], F32, name="warm")
        nc.vector.memset(zero1[:], 0.0)
        nc.scalar.activation(out=warm[:], in_=zero1[:], func=ACT.Sin)

        NT = TPP * 32
        pos_f = const.tile([P, TPP], F32, name="pos_f")
        freq = const.tile([P, 32], F32, name="freq")
        ang = const.tile([P, NT], F32, name="ang")
        turns_i = const.tile([P, NT], I32, name="turns_i")
        turns = const.tile([P, NT], F32, name="turns")
        red1 = const.tile([P, NT], F32, name="red1")
        red = const.tile([P, NT], F32, name="red")
        nabs = const.tile([P, NT], F32, name="nabs")
        carg = const.tile([P, NT], F32, name="carg")
        sin_h = const.tile([P, NT], F32, name="sin_h")
        cos_h = const.tile([P, NT], F32, name="cos_h")
        sq_h = const.tile([P, NT], F32, name="sq_h")
        sin_half = const.tile([P, NT], F32, name="sin_half")
        sign2 = const.tile([P, 2], F32, name="sign2")
        tab = const.tile([P, 4, 2, 2, 64], F32, name="tab")

        nc.vector.tensor_copy(out=pos_f[:], in_=pos_i[:])
        nc.vector.memset(freq[:, 0:1], 1.0)
        nc.vector.memset(sign2[:, 0:1], 2.0)
        nc.vector.memset(sign2[:, 1:2], -2.0)
        w = 1
        while w < 32:
            nc.vector.tensor_scalar(
                out=freq[:, w : 2 * w], in0=freq[:, 0:w], scalar1=THETA ** (-w / 32.0), scalar2=None, op0=ALU.mult
            )
            w *= 2
        nc.vector.tensor_tensor(
            out=ang[:].rearrange("p (j i) -> p j i", j=TPP),
            in0=pos_f[:].unsqueeze(2).to_broadcast([P, TPP, 32]),
            in1=freq[:].unsqueeze(1).to_broadcast([P, TPP, 32]),
            op=ALU.mult,
        )
        nc.vector.tensor_scalar(
            out=turns_i[:], in0=ang[:], scalar1=1.0 / TWO_PI, scalar2=0.25, op0=ALU.mult, op1=ALU.add
        )
        nc.vector.tensor_copy(out=turns[:], in_=turns_i[:])
        nc.vector.scalar_tensor_tensor(out=red1[:], in0=turns[:], scalar=-C1, in1=ang[:], op0=ALU.mult, op1=ALU.add)
        nc.vector.scalar_tensor_tensor(out=red[:], in0=turns[:], scalar=-C2, in1=red1[:], op0=ALU.mult, op1=ALU.add)
        nc.vector.scalar_tensor_tensor(out=nabs[:], in0=red[:], scalar=-1.0, in1=red[:], op0=ALU.mult, op1=ALU.min)
        nc.vector.tensor_scalar(
            out=carg[:], in0=nabs[:], scalar1=0.5, scalar2=0.5 * math.pi, op0=ALU.mult, op1=ALU.add
        )
        nc.scalar.activation(out=sin_h[:], in_=red[:], func=ACT.Sin, scale=0.5)
        nc.scalar.activation(out=cos_h[:], in_=carg[:], func=ACT.Sin)
        nc.scalar.activation(out=sq_h[:], in_=sin_h[:], func=ACT.Square)

        def transposes(n):
            xt, off = x_of_pair[n]
            xw = xt[:].bitcast(F32)
            banks = []
            for a in range(2):
                tp = psum.tile([P, 4, P], F32, name="tp%d" % a, tag="tp%d" % a, bufs=1)
                for v in range(4):
                    c0 = (off + a) * 512 + v * P
                    nc.tensor.transpose(tp[:, v, :], xw[:, c0 : c0 + P], ident[:])
                banks.append(tp)
            return banks

        def evacuate(banks):
            xg = work.tile([P, 2048], BF16, name="xg", tag="xg", align_bytes=64)
            xgw = xg[:].bitcast(F32).rearrange("p (a g r u) -> p a g r u", a=2, g=2, r=P, u=2)
            for a in range(2):
                nc.scalar.copy(out=xgw[:, a], in_=banks[a][:].rearrange("p (g u) r -> p g r u", u=2))
            return xg

        def quantise_x(xg):
            xc = work.tile([P, 512], U32, name="xc", tag="xc", align_bytes=64)
            xs = work.tile([P, 512], U8, name="xs", tag="xs", align_bytes=64)
            nc.vector.quantize_mx(out=xc[:].bitcast(FP8X4), scales=xs[:], in_=xg[:])
            return xc, xs

        xg_of = {}
        xq_of = {}

        wg = const.tile([P, 2 * 768 * 4], BF16, name="wg", align_bytes=64)
        wg_v = wg[:].rearrange("p (g c t) -> p g c t", g=2, c=768, t=4)
        wc = const.tile([P, 2, 768], U32, name="wc", align_bytes=64)
        ws = const.tile([P, 2, 768], U8, name="ws", align_bytes=64)

        def regroup_q(copy, g, s):
            src = wq_raw[g][:].rearrange("p (t h s f) -> p s h f t", t=4, h=4, s=2, f=64)
            copy(out=wg_v[:, g, s * 256 : (s + 1) * 256, :].rearrange("p (h f) t -> p h f t", h=4), in_=src[:, s])

        def regroup_kv(raw, c0):
            nc.vector.tensor_copy(
                out=wg_v[:, :, c0 : c0 + P, :], in_=raw[:].rearrange("p (g t c) -> p g c t", g=2, t=4, c=P)
            )

        def quantise_w(g, c0, c1):
            nc.vector.quantize_mx(
                out=wc[:, g, c0:c1].bitcast(FP8X4),
                scales=ws[:, g, c0:c1],
                in_=wg_v[:, g, c0:c1, :].rearrange("p c t -> p (c t)"),
            )

        regroup_q(nc.vector.tensor_copy, 0, 0)
        regroup_q(nc.scalar.copy, 0, 1)
        nc.vector.tensor_tensor(out=sin_half[:], in0=sin_h[:], in1=cos_h[:], op=ALU.mult)
        regroup_q(nc.vector.tensor_copy, 1, 0)
        regroup_q(nc.scalar.copy, 1, 1)
        xg_of[0] = evacuate(transposes(0))
        xg_of[1] = evacuate(transposes(1))
        quantise_w(0, 0, 256)
        quantise_w(1, 0, 256)
        quantise_w(0, 256, 512)
        quantise_w(1, 256, 512)
        nc.vector.tensor_tensor(
            out=tab[:, :, 1].rearrange("p q a (i e) -> p q (a i) e", e=2),
            in0=sin_half[:].rearrange("p (q x) -> p q x", q=4).unsqueeze(3).to_broadcast([P, 4, 64, 2]),
            in1=sign2[:].unsqueeze(1).unsqueeze(1).to_broadcast([P, 4, 64, 2]),
            op=ALU.mult,
        )
        xq_of[0] = quantise_x(xg_of[0])
        regroup_kv(wk_raw, 512)
        xq_of[1] = quantise_x(xg_of[1])
        regroup_kv(wv_raw, 640)
        quantise_w(0, 512, 768)
        quantise_w(1, 512, 768)
        nc.vector.tensor_scalar(
            out=tab[:, :, 0].rearrange("p q a (i e) -> p q (a i) e", e=2),
            in0=sq_h[:].rearrange("p (q x) -> p q x", q=4).unsqueeze(3).to_broadcast([P, 4, 64, 2]),
            scalar1=-2.0,
            scalar2=1.0,
            op0=ALU.mult,
            op1=ALU.add,
        )

        banks_of = {}
        q_tile_of = {}
        kv_tile_of = {}

        def mx(n, bank, c0):
            xc, xs = xq_of[n]
            for a in range(2):
                for g in range(2):
                    blk = slice((a * 2 + g) * P, (a * 2 + g + 1) * P)
                    nc.tensor.matmul_mx(
                        out=bank[:, a * 256 : (a + 1) * 256],
                        lhsT=xc[:, blk].bitcast(FP8X4),
                        lhsT_scale=xs[:, blk],
                        rhs=wc[:, g, c0 : c0 + 256].bitcast(FP8X4),
                        rhs_scale=ws[:, g, c0 : c0 + 256],
                        start=(g == 0),
                        stop=(g == 1),
                    )

        def out_tiles(n):
            for grp in Q_GROUPS:
                if grp[0] == n:
                    qo = outp.tile([P, len(grp) * 8, P], F32, name="qo", tag="qo")
                    for k, m in enumerate(grp):
                        q_tile_of[m] = (qo, k, grp)
            for grp in KV_GROUPS:
                if grp[0] == n:
                    ko = outp.tile([P, len(grp) * 2, P], F32, name="ko", tag="ko", bufs=3)
                    vo = outp.tile([P, len(grp) * 2, P], F32, name="vo", tag="vo", bufs=3)
                    for k, m in enumerate(grp):
                        kv_tile_of[m] = (ko, vo, k, grp)

        rope_tmp = {}

        def rope_q_mul(n):
            t12 = rope.tile([P, 2, 512], F32, name="t12q", tag="t12q")
            nc.vector.tensor_tensor(
                out=t12[:].rearrange("p c (a h f) -> p c a h f", a=2, h=4),
                in0=banks_of[n][0][:]
                .rearrange("p (a h f) -> p a h f", a=2, h=4)
                .unsqueeze(1)
                .to_broadcast([P, 2, 2, 4, 64]),
                in1=tab[:, n % 4].unsqueeze(3).to_broadcast([P, 2, 2, 4, 64]),
                op=ALU.mult,
            )
            rope_tmp[("q", n)] = t12

        def rope_q_add(n, eng, m0=0, m1=8):
            qo, k, grp = q_tile_of[n]
            t12 = rope_tmp[("q", n)]
            eng.tensor_tensor(
                out=qo[:, 8 * k + m0 : 8 * k + m1, 0:64].rearrange("p m (i e) -> p m i e", e=2),
                in0=t12[:, 0].rearrange("p (m i e) -> p m i e", m=8, e=2)[:, m0:m1],
                in1=t12[:, 1].rearrange("p (m i e) -> p m i e", m=8, e=2)[:, m0:m1, :, ::-1],
                op=ALU.add,
            )

        def store_q_tile(n, a):
            qo, k, grp = q_tile_of[n]
            b, j = n // 4, 2 * (n % 4) + a
            dst = out_0[b].rearrange("(p j) h d -> p (j h d)", j=TPP)
            nc.sync.dma_start(
                out=dst[:, j * 512 : (j + 1) * 512],
                in_=qo[:, 8 * k + 4 * a : 8 * k + 4 * a + 4, :].rearrange("p m d -> p (m d)"),
            )

        def rope_k_mul(n):
            t12 = rope.tile([P, 2, 2, 64], F32, name="t12k", tag="t12k")
            nc.vector.tensor_tensor(
                out=t12[:],
                in0=banks_of[n][2][:]
                .rearrange("p (a s f) -> p a s f", a=2, s=4)[:, :, 0, :]
                .unsqueeze(1)
                .to_broadcast([P, 2, 2, 64]),
                in1=tab[:, n % 4],
                op=ALU.mult,
            )
            rope_tmp[("k", n)] = t12
            ko, vo, k, grp = kv_tile_of[n]
            nc.vector.tensor_copy(
                out=ko[:, 2 * k : 2 * k + 2, 64:128],
                in_=banks_of[n][2][:].rearrange("p (a s f) -> p a s f", a=2, s=4)[:, :, 1, :],
            )

        def rope_k_add(n):
            ko, vo, k, grp = kv_tile_of[n]
            t12 = rope_tmp[("k", n)]
            nc.vector.tensor_tensor(
                out=ko[:, 2 * k : 2 * k + 2, 0:64].rearrange("p a (i e) -> p a i e", e=2),
                in0=t12[:, 0].rearrange("p a (i e) -> p a i e", e=2),
                in1=t12[:, 1].rearrange("p a (i e) -> p a i e", e=2)[:, :, :, ::-1],
                op=ALU.add,
            )

        def copy_q(n):
            qo, k, grp = q_tile_of[n]
            nc.scalar.copy(
                out=qo[:, 8 * k : 8 * k + 8, 64:128], in_=banks_of[n][1][:].rearrange("p (m f) -> p m f", m=8)
            )

        def copy_kv(n):
            bank_k = banks_of[n][2]
            ko, vo, k, grp = kv_tile_of[n]
            nc.scalar.copy(
                out=vo[:, 2 * k : 2 * k + 2, :], in_=bank_k[:].rearrange("p (a s f) -> p a s f", a=2, s=2)[:, :, 1, :]
            )

        def store_q(n):
            qo, k, grp = q_tile_of[n]
            if grp[-1] != n:
                return
            b, j0 = grp[0] // 4, 2 * (grp[0] % 4)
            dst = out_0[b].rearrange("(p j) h d -> p (j h d)", j=TPP)
            nc.sync.dma_start(
                out=dst[:, j0 * 512 : (j0 + 2 * len(grp)) * 512], in_=qo[:].rearrange("p m d -> p (m d)")
            )

        def store_kv(n):
            ko, vo, k, grp = kv_tile_of[n]
            if grp[-1] != n:
                return
            b, j0 = grp[0] // 4, 2 * (grp[0] % 4)
            for dram, sb in ((out_1, ko), (out_2, vo)):
                dst = dram[b].rearrange("(p j) o d -> p (j o d)", j=TPP)
                nc.sync.dma_start(
                    out=dst[:, j0 * P : (j0 + 2 * len(grp)) * P], in_=sb[:].rearrange("p m d -> p (m d)")
                )

        def new_banks(n):
            out_tiles(n)
            bank_r = psum.tile([P, 512], F32, name="bank_r", tag="bank_r")
            bank_p = psum.tile([P, 512], F32, name="bank_p", tag="bank_p")
            bank_k = psum.tile([P, 512], F32, name="bank_k", tag="bank_k")
            banks_of[n] = (bank_r, bank_p, bank_k)

        def mx_q(n):
            mx(n, banks_of[n][0], 0)
            mx(n, banks_of[n][1], 256)
            copy_q(n)

        def mx_kv(n):
            mx(n, banks_of[n][2], 512)
            copy_kv(n)

        def ahead(n):
            if n < NPAIR:
                xg_of[n] = evacuate(transposes(n))

        def vector_part(n):
            rope_q_mul(n)
            rope_q_add(n, nc.gpsimd)
            store_q(n)
            if n + 2 < NPAIR:
                xq_of[n + 2] = quantise_x(xg_of[n + 2])
            if n > 0:
                rope_k_add(n - 1)
                store_kv(n - 1)
            rope_k_mul(n)

        new_banks(0)
        new_banks(1)
        mx_q(0)
        mx_q(1)
        ahead(2)
        mx_kv(0)
        mx_kv(1)
        ahead(3)
        vector_part(0)
        vector_part(1)
        for n in range(2, NPAIR - 1):
            new_banks(n)
            mx_q(n)
            ahead(n + 2)
            mx_kv(n)
            vector_part(n)

        last = NPAIR - 1
        new_banks(last)
        mx_kv(last)
        mx_q(last)
        rope_k_add(last - 1)
        store_kv(last - 1)
        rope_k_mul(last)
        rope_k_add(last)
        store_kv(last)
        rope_q_mul(last)
        for a in range(2):
            rope_q_add(last, nc.vector, 4 * a, 4 * a + 4)
            store_q_tile(last, a)
